import numpy as np
import ml_dtypes


def mxq(x, axis, fmt="e4m3"):
    dtype, down = {"e4m3": (ml_dtypes.float8_e4m3fn, 7), "e5m2": (ml_dtypes.float8_e5m2, 14)}[fmt]
    v = np.moveaxis(np.asarray(x, np.float32).astype(ml_dtypes.bfloat16).astype(np.float64), axis, -1)
    blocks = v.reshape(v.shape[:-1] + (-1, 32))
    amax = np.abs(blocks).max(-1, keepdims=True)
    byte = np.maximum(np.where(amax > 0, np.frexp(amax)[1] - 1 + 127, 0) - down, 1)
    scale = np.exp2(byte - 127.0)
    codes = (blocks / scale).astype(np.float32).astype(dtype).astype(np.float64)
    return np.moveaxis((codes * scale).reshape(v.shape), -1, axis)


WIDE = False


def mx_kscale(k):
    if not WIDE:
        return np.ones(k)
    levels = np.array([10, -10, 5, -5, 0])
    a = np.random.permutation(np.resize(levels, k // 512 * 4)).reshape(k // 512, 4)
    idx = np.arange(k)
    return np.exp2(a[idx // 512, idx % 128 // 32])


BF16 = ml_dtypes.bfloat16


def bf(x):
    return np.asarray(x, np.float32).astype(BF16)


def f64(x):
    return np.asarray(x).astype(np.float64)


TOKENS, IN_FEATURES, OUT_FEATURES = 1024, 2048, 2048


def setup_inputs():
    a = np.sqrt(6.0 / (IN_FEATURES + OUT_FEATURES))
    s = mx_kscale(IN_FEATURES)
    return {"input": bf(np.random.standard_normal((TOKENS, IN_FEATURES)) * 4.0 / np.sqrt(IN_FEATURES) * (s / s.min())[None, :]),
            "weight": bf(np.random.uniform(-a, a, (OUT_FEATURES, IN_FEATURES)) / (s ** 4)[None, :])}


def reference(input, weight):
    w = f64(weight)
    abs_w = np.abs(w)
    abs_mean = np.mean(abs_w)
    w_ternary = np.where(abs_w > abs_mean, np.sign(w), np.zeros_like(w))
    return mxq(f64(input), 1, "e4m3") @ mxq(w_ternary, 1, "e4m3").T

@@ -1,0 +1,272 @@
+from contextlib import ExitStack
+
+import concourse.mybir as mybir
+from concourse.masks import make_identity
+
+F32 = mybir.dt.float32
+BF16 = mybir.dt.bfloat16
+I32 = mybir.dt.int32
+U32 = mybir.dt.uint32
+U8 = mybir.dt.uint8
+FP8X4 = mybir.dt.float8_e4m3fn_x4
+ALU = mybir.AluOpType
+AX = mybir.AxisListType
+ACT = mybir.ActivationFunctionType
+
+P = 128
+TOKENS, K, OUTF = 1024, 2048, 2048
+FLOPS = 2 * TOKENS * K * OUTF
+NG = K // 512
+NOB = OUTF // 512
+NI = TOKENS // P
+NCH = OUTF // P
+MAG_BITS = 0x7FFF7FFF
+SIGN_BITS = -2147450880
+NAT_BUFS = 10
+TR_BANKS = 6
+S_SUM_FROM = 14
+BLOCKS = ((0, 0, 512), (1, 0, 512), (2, 0, 512), (3, 0, 256), (3, 256, 256))
+LEAD = 5
+X_BANKS = ((2, 3), (4, 5), (0, 1), (6, 7), (2, 3), (4, 5), (6, 7), (4, 5))
+
+
+def tile_ternarylinear_kernel(tc, x, weight, out):
+    nc = tc.nc
+    with ExitStack() as ctx:
+        ctx.enter_context(tc.manual_schedule())
+        const = ctx.enter_context(tc.tile_pool(name="const", bufs=1))
+        keep = ctx.enter_context(tc.tile_pool(name="keep", bufs=1))
+        nat = ctx.enter_context(tc.tile_pool(name="nat", bufs=NAT_BUFS))
+        psum = ctx.enter_context(tc.psum_pool(name="psum", bufs=1))
+
+        ident = const.tile([P, P], F32, name="ident")
+        make_identity(nc, ident[:])
+        ones_bf = const.tile([P, P], BF16, name="ones_bf")
+        nc.vector.memset(ones_bf[:], 1.0)
+        ones_f = const.tile([P, P], F32, name="ones_f")
+        nc.vector.memset(ones_f[:], 1.0)
+        partv = const.tile([P, NCH], F32, name="partv")
+        parts = const.tile([P, NCH], F32, name="parts")
+        nc.vector.memset(parts[:], 0.0)
+        junk = const.tile([P, 512], F32, name="junk")
+        nc.scalar.activation(out=junk[:, 0:1], in_=parts[:, 0:1], func=ACT.Abs)
+        tsum = const.tile([P, 1], F32, name="tsum")
+        vsum = const.tile([P, 1], F32, name="vsum")
+        mean = const.tile([P, 1], F32, name="mean")
+
+        raw = [keep.tile([P, 4096], F32, name="raw%d" % b, align_bytes=64) for b in range(NOB)]
+        mag = [keep.tile([P, 4096], F32, name="mag%d" % b, align_bytes=64) for b in range(NOB)]
+        wcod = [keep.tile([P, 2048], U32, name="wcod%d" % b, align_bytes=64) for b in range(NOB)]
+        wpl = [keep.tile([P, 2048], U8, name="wpl%d" % b, align_bytes=64) for b in range(NOB)]
+        xcod = [keep.tile([P, 512], U32, name="xcod%d" % i, align_bytes=64) for i in range(NI)]
+        xpl = [keep.tile([P, 512], U8, name="xpl%d" % i, align_bytes=64) for i in range(NI)]
+        banks = [psum.tile([P, 512], F32, name="bank%d" % b) for b in range(8)]
+
+        def load(rows):
+            t = nat.tile([P, K], BF16, name="natt", tag="nat", align_bytes=64)
+            nc.sync.dma_start(out=t[:], in_=rows)
+            return t
+
+        def transposes(src, pair):
+            words = src[:].bitcast(F32)
+            for j in range(8):
+                nc.tensor.transpose(
+                    banks[pair[j // 4]][:, (j % 4) * P : (j % 4 + 1) * P], words[:, j * P : (j + 1) * P], ident[:]
+                )
+
+        def exits(dst, pair, copy):
+            for h in range(2):
+                copy(
+                    out=dst[:, 2 * h : 2 * h + 2, :, :],
+                    in_=banks[pair[h]][:].rearrange("p (g u o) -> p g o u", g=2, u=2),
+                )
+
+        def chunk_view(tile_ap, dtype, c4, per_col):
+            return tile_ap[:].bitcast(dtype).rearrange("p (g e) -> p g e", g=NG)[
+                :, :, c4 * P * per_col : (c4 + 1) * P * per_col
+            ]
+
+        wn = {}
+        xn = {}
+        for c in range(NAT_BUFS):
+            wn[c] = load(weight[c * P : (c + 1) * P, :])
+        n_tmm = 2 * NCH
+        tmm = [0]
+
+        def tensor_sum(c):
+            ob, c4 = c // 4, c % 4
+            for g in range(2):
+                nc.tensor.matmul(
+                    out=banks[6][:],
+                    lhsT=ones_bf[:],
+                    rhs=mag[ob][:].bitcast(BF16)[:, g * 2048 + c4 * 512 : g * 2048 + (c4 + 1) * 512],
+                    start=(tmm[0] == 0),
+                    stop=(tmm[0] == n_tmm - 1),
+                )
+                tmm[0] += 1
+
+        def vector_sum(c):
+            g1 = NG if c < S_SUM_FROM else NG - 1
+            part = chunk_view(mag[c // 4], BF16, c % 4, 4)[:, 2:g1, :]
+            nc.vector.tensor_scalar(
+                out=part, in0=part, scalar1=1.0, scalar2=None, op0=ALU.mult, op1=ALU.add, accum_out=partv[:, c : c + 1]
+            )
+
+        def scalar_sum(c):
+            nc.scalar.activation(
+                out=junk[:].bitcast(BF16)[:, 0:512],
+                in_=chunk_view(raw[c // 4], BF16, c % 4, 4)[:, NG - 1, :],
+                func=ACT.Abs,
+                accum_out=parts[:, c - S_SUM_FROM : c - S_SUM_FROM + 1],
+            )
+
+        for c in range(NCH):
+            ob, c4 = c // 4, c % 4
+            pair = ((2 * c) % TR_BANKS, (2 * c + 1) % TR_BANKS)
+            transposes(wn[c], pair)
+            if c >= 2:
+                tensor_sum(c - 2)
+            exits(raw[ob][:].rearrange("p (g o u) -> p g o u", g=NG, u=2)[:, :, c4 * P : (c4 + 1) * P, :], pair, nc.scalar.copy)
+            nc.vector.tensor_scalar(
+                out=chunk_view(mag[ob], I32, c4, 2),
+                in0=chunk_view(raw[ob], I32, c4, 2),
+                scalar1=MAG_BITS,
+                scalar2=None,
+                op0=ALU.bitwise_and,
+            )
+            if c >= 1:
+                vector_sum(c - 1)
+            nxt = c + NAT_BUFS
+            if nxt < NCH:
+                wn[nxt] = load(weight[nxt * P : (nxt + 1) * P, :])
+            elif nxt < NCH + NI:
+                xn[nxt - NCH] = load(x[(nxt - NCH) * P : (nxt - NCH + 1) * P, :])
+
+        xg = {}
+
+        def x_turn(i):
+            x_transposes(i)
+            x_exits(i, nc.scalar.copy)
+
+        def x_transposes(i):
+            transposes(xn[i], X_BANKS[i])
+
+        def x_exits(i, copy):
+            xg[i] = nat.tile([P, 1024], F32, name="xgt", tag="nat", align_bytes=64)
+            exits(xg[i][:].rearrange("p (g o u) -> p g o u", g=NG, u=2), X_BANKS[i], copy)
+
+        x_ready = []
+        t_ready = []
+        count = {}
+        nxt_j = [0] * NI
+
+        def issue(last):
+            for i in x_ready:
+                top = len(t_ready) if (i < LEAD or last or len(t_ready) < NG) else len(t_ready) - 1
+                while nxt_j[i] < top:
+                    one_pass(nxt_j[i], i)
+                    nxt_j[i] += 1
+
+        def leave(b, i, copy):
+            ob, o0, w = BLOCKS[b]
+            st = nat.tile([P, 512], F32, name="stage", tag="nat", align_bytes=64)
+            copy(out=st[:, 0:w], in_=banks[i][:, 0:w])
+            nc.sync.dma_start(out=out[i * P : (i + 1) * P, ob * 512 + o0 : ob * 512 + o0 + w], in_=st[:, 0:w])
+
+        def one_pass(j, i):
+            b, g = j // NG, j % NG
+            ob, o0, w = BLOCKS[b]
+            n = count.get((b, i), 0)
+            nc.tensor.matmul_mx(
+                out=banks[i][:, 0:w],
+                lhsT=xcod[i][:, g * P : (g + 1) * P].bitcast(FP8X4),
+                lhsT_scale=xpl[i][:, g * P : (g + 1) * P],
+                rhs=wcod[ob][:, g * 512 + o0 : g * 512 + o0 + w].bitcast(FP8X4),
+                rhs_scale=wpl[ob][:, g * 512 + o0 : g * 512 + o0 + w],
+                start=(n == 0),
+                stop=(n == NG - 1),
+            )
+            count[(b, i)] = n + 1
+            if n == NG - 1:
+                if b == len(BLOCKS) - 1 and i % 2 == 1:
+                    leave(b, i, nc.vector.tensor_copy)
+                else:
+                    leave(b, i, nc.scalar.copy)
+
+        def x_quant(i):
+            nc.vector.quantize_mx(out=xcod[i][:].bitcast(FP8X4), scales=xpl[i][:], in_=xg[i][:].bitcast(BF16))
+            x_ready.append(i)
+            issue(False)
+
+        def mask(j):
+            ob, o0, w = BLOCKS[j // NG]
+            a = (j % NG) * 2048 + 4 * o0
+            v = mag[ob][:].bitcast(BF16)[:, a : a + 4 * w]
+            nc.vector.tensor_scalar(out=v, in0=v, scalar1=mean[:, 0:1], scalar2=None, op0=ALU.is_gt)
+
+        def merge(j):
+            ob, o0, w = BLOCKS[j // NG]
+            a = (j % NG) * 1024 + 2 * o0
+            r = raw[ob][:].bitcast(I32)[:, a : a + 2 * w]
+            nc.vector.scalar_tensor_tensor(
+                out=r,
+                in0=r,
+                scalar=SIGN_BITS,
+                in1=mag[ob][:].bitcast(I32)[:, a : a + 2 * w],
+                op0=ALU.bitwise_and,
+                op1=ALU.bitwise_or,
+            )
+
+        def t_quant(j):
+            ob, o0, w = BLOCKS[j // NG]
+            g = j % NG
+            nc.vector.quantize_mx(
+                out=wcod[ob][:, g * 512 + o0 : g * 512 + o0 + w].bitcast(FP8X4),
+                scales=wpl[ob][:, g * 512 + o0 : g * 512 + o0 + w],
+                in_=raw[ob][:].bitcast(BF16)[:, g * 2048 + 4 * o0 : g * 2048 + 4 * (o0 + w)],
+            )
+            t_ready.append(j)
+            issue(j == len(BLOCKS) * NG - 1)
+
+        for c in range(S_SUM_FROM, NCH):
+            scalar_sum(c)
+        tensor_sum(NCH - 2)
+        x_transposes(0)
+        vector_sum(NCH - 1)
+        tensor_sum(NCH - 1)
+        nc.scalar.activation(out=junk[:], in_=banks[6][:], func=ACT.Copy, accum_out=tsum[:])
+        x_turn(1)
+        x_exits(0, nc.vector.tensor_copy)
+        nc.tensor.matmul(out=banks[7][:, 0:NCH], lhsT=ones_f[:], rhs=partv[:], start=True, stop=True)
+        nc.tensor.matmul(out=banks[7][:, NCH : 2 * NCH], lhsT=ones_f[:], rhs=parts[:], start=True, stop=True)
+        nc.vector.tensor_reduce(out=vsum[:], in_=banks[7][:, 0 : 2 * NCH], axis=AX.X, op=ALU.add)
+        nc.vector.tensor_scalar(
+            out=mean[:], in0=vsum[:], scalar1=tsum[:, 0:1], scalar2=1.0 / (OUTF * K), op0=ALU.add, op1=ALU.mult
+        )
+        for i in range(2, 7):
+            x_turn(i)
+        nj = len(BLOCKS) * NG
+        mask(0)
+        x_quant(0)
+        merge(0)
+        x_quant(1)
+        t_quant(0)
+        x_quant(2)
+        x_quant(3)
+        x_turn(7)
+        mask(1)
+        x_quant(4)
+        merge(1)
+        x_quant(5)
+        t_quant(1)
+        x_quant(6)
+        mask(2)
+        x_quant(7)
+        merge(2)
+        mask(3)
+        t_quant(2)
+        for j in range(3, nj):
+            merge(j)
+            if j + 1 < nj:
+                mask(j + 1)
+            t_quant(j)

@@ -33,7 +33,6 @@ X_BANKS = ((2, 3), (4, 5), (0, 1), (6, 7), (2, 3), (4, 5), (6, 7), (4, 5))
 def tile_ternarylinear_kernel(tc, x, weight, out):
     nc = tc.nc
     with ExitStack() as ctx:
-        ctx.enter_context(tc.manual_schedule())
         const = ctx.enter_context(tc.tile_pool(name="const", bufs=1))
         keep = ctx.enter_context(tc.tile_pool(name="keep", bufs=1))
         nat = ctx.enter_context(tc.tile_pool(name="nat", bufs=NAT_BUFS))

@@ -21,10 +21,9 @@ NOB = OUTF // 512
 NI = TOKENS // P
 NCH = OUTF // P
 MAG_BITS = 0x7FFF7FFF
-SIGN_BITS = -2147450880
 NAT_BUFS = 10
 TR_BANKS = 6
-S_SUM_FROM = 14
+T_SLICES = 3
 BLOCKS = ((0, 0, 512), (1, 0, 512), (2, 0, 512), (3, 0, 256), (3, 256, 256))
 LEAD = 5
 X_BANKS = ((2, 3), (4, 5), (0, 1), (6, 7), (2, 3), (4, 5), (6, 7), (4, 5))
@@ -45,10 +44,8 @@ def tile_ternarylinear_kernel(tc, x, weight, out):
         ones_f = const.tile([P, P], F32, name="ones_f")
         nc.vector.memset(ones_f[:], 1.0)
         partv = const.tile([P, NCH], F32, name="partv")
-        parts = const.tile([P, NCH], F32, name="parts")
-        nc.vector.memset(parts[:], 0.0)
         junk = const.tile([P, 512], F32, name="junk")
-        nc.scalar.activation(out=junk[:, 0:1], in_=parts[:, 0:1], func=ACT.Abs)
+        nc.scalar.activation(out=junk[:, 0:1], in_=ones_f[:, 0:1], func=ACT.Copy)
         tsum = const.tile([P, 1], F32, name="tsum")
         vsum = const.tile([P, 1], F32, name="vsum")
         mean = const.tile([P, 1], F32, name="mean")
@@ -89,12 +86,12 @@ def tile_ternarylinear_kernel(tc, x, weight, out):
         xn = {}
         for c in range(NAT_BUFS):
             wn[c] = load(weight[c * P : (c + 1) * P, :])
-        n_tmm = 2 * NCH
+        n_tmm = T_SLICES * NCH
         tmm = [0]
 
         def tensor_sum(c):
             ob, c4 = c // 4, c % 4
-            for g in range(2):
+            for g in range(T_SLICES):
                 nc.tensor.matmul(
                     out=banks[6][:],
                     lhsT=ones_bf[:],
@@ -105,19 +102,14 @@ def tile_ternarylinear_kernel(tc, x, weight, out):
                 tmm[0] += 1
 
         def vector_sum(c):
-            g1 = NG if c < S_SUM_FROM else NG - 1
-            part = chunk_view(mag[c // 4], BF16, c % 4, 4)[:, 2:g1, :]
+            part = chunk_view(mag[c // 4], BF16, c % 4, 4)[:, T_SLICES:NG, :]
             nc.vector.tensor_scalar(
                 out=part, in0=part, scalar1=1.0, scalar2=None, op0=ALU.mult, op1=ALU.add, accum_out=partv[:, c : c + 1]
             )
 
-        def scalar_sum(c):
-            nc.scalar.activation(
-                out=junk[:].bitcast(BF16)[:, 0:512],
-                in_=chunk_view(raw[c // 4], BF16, c % 4, 4)[:, NG - 1, :],
-                func=ACT.Abs,
-                accum_out=parts[:, c - S_SUM_FROM : c - S_SUM_FROM + 1],
-            )
+        def half_sign(c):
+            v = chunk_view(raw[c // 4], BF16, c % 4, 4)
+            nc.vector.tensor_scalar(out=v, in0=v, scalar1=0.0, scalar2=0.5, op0=ALU.is_ge, op1=ALU.subtract)
 
         for c in range(NCH):
             ob, c4 = c // 4, c % 4
@@ -135,6 +127,7 @@ def tile_ternarylinear_kernel(tc, x, weight, out):
             )
             if c >= 1:
                 vector_sum(c - 1)
+                half_sign(c - 1)
             nxt = c + NAT_BUFS
             if nxt < NCH:
                 wn[nxt] = load(weight[nxt * P : (nxt + 1) * P, :])
@@ -201,20 +194,13 @@ def tile_ternarylinear_kernel(tc, x, weight, out):
             ob, o0, w = BLOCKS[j // NG]
             a = (j % NG) * 2048 + 4 * o0
             v = mag[ob][:].bitcast(BF16)[:, a : a + 4 * w]
-            nc.vector.tensor_scalar(out=v, in0=v, scalar1=mean[:, 0:1], scalar2=None, op0=ALU.is_gt)
+            nc.vector.tensor_scalar(out=v, in0=v, scalar1=mean[:, 0:1], scalar2=2.0, op0=ALU.is_gt, op1=ALU.mult)
 
         def merge(j):
             ob, o0, w = BLOCKS[j // NG]
-            a = (j % NG) * 1024 + 2 * o0
-            r = raw[ob][:].bitcast(I32)[:, a : a + 2 * w]
-            nc.vector.scalar_tensor_tensor(
-                out=r,
-                in0=r,
-                scalar=SIGN_BITS,
-                in1=mag[ob][:].bitcast(I32)[:, a : a + 2 * w],
-                op0=ALU.bitwise_and,
-                op1=ALU.bitwise_or,
-            )
+            a = (j % NG) * 2048 + 4 * o0
+            r = raw[ob][:].bitcast(BF16)[:, a : a + 4 * w]
+            nc.vector.tensor_tensor(out=r, in0=mag[ob][:].bitcast(BF16)[:, a : a + 4 * w], in1=r, op=ALU.mult)
 
         def t_quant(j):
             ob, o0, w = BLOCKS[j // NG]
@@ -227,8 +213,6 @@ def tile_ternarylinear_kernel(tc, x, weight, out):
             t_ready.append(j)
             issue(j == len(BLOCKS) * NG - 1)
 
-        for c in range(S_SUM_FROM, NCH):
-            scalar_sum(c)
         tensor_sum(NCH - 2)
         x_transposes(0)
         vector_sum(NCH - 1)
@@ -237,13 +221,13 @@ def tile_ternarylinear_kernel(tc, x, weight, out):
         x_turn(1)
         x_exits(0, nc.vector.tensor_copy)
         nc.tensor.matmul(out=banks[7][:, 0:NCH], lhsT=ones_f[:], rhs=partv[:], start=True, stop=True)
-        nc.tensor.matmul(out=banks[7][:, NCH : 2 * NCH], lhsT=ones_f[:], rhs=parts[:], start=True, stop=True)
-        nc.vector.tensor_reduce(out=vsum[:], in_=banks[7][:, 0 : 2 * NCH], axis=AX.X, op=ALU.add)
+        nc.vector.tensor_reduce(out=vsum[:], in_=banks[7][:, 0:NCH], axis=AX.X, op=ALU.add)
         nc.vector.tensor_scalar(
             out=mean[:], in0=vsum[:], scalar1=tsum[:, 0:1], scalar2=1.0 / (OUTF * K), op0=ALU.add, op1=ALU.mult
         )
         for i in range(2, 7):
             x_turn(i)
+        half_sign(NCH - 1)
         nj = len(BLOCKS) * NG
         mask(0)
         x_quant(0)

@@ -17,24 +17,33 @@ P = 128
 TOKENS, K, OUTF = 1024, 2048, 2048
 FLOPS = 2 * TOKENS * K * OUTF
 NG = K // 512
-NOB = OUTF // 512
 NI = TOKENS // P
 NCH = OUTF // P
 MAG_BITS = 0x7FFF7FFF
-NAT_BUFS = 10
+SIGN_BITS = -2147450880
+MANUAL = True
+NAT_BUFS = 8
 TR_BANKS = 6
-T_SLICES = 3
-BLOCKS = ((0, 0, 512), (1, 0, 512), (2, 0, 512), (3, 0, 256), (3, 256, 256))
-LEAD = 5
-X_BANKS = ((2, 3), (4, 5), (0, 1), (6, 7), (2, 3), (4, 5), (6, 7), (4, 5))
+BLOCK_CHUNKS = (1, 1, 2, 2, 2, 2, 2, 2, 1, 1)
+T_SLICES = 2
+SUM_LAG = 2
+MX_BANKS = (0, 1, 2, 3)
+X_BANKS = ((2, 3), (4, 5), (0, 1), (6, 7), (4, 5), (6, 7), (4, 5), (6, 7))
 
 
 def tile_ternarylinear_kernel(tc, x, weight, out):
     nc = tc.nc
+    nb = len(BLOCK_CHUNKS)
+    first = [sum(BLOCK_CHUNKS[:b]) for b in range(nb)]
+    width = [P * n for n in BLOCK_CHUNKS]
+    block_of = [b for b in range(nb) for q in range(BLOCK_CHUNKS[b])]
     with ExitStack() as ctx:
+        if MANUAL:
+            ctx.enter_context(tc.manual_schedule())
         const = ctx.enter_context(tc.tile_pool(name="const", bufs=1))
         keep = ctx.enter_context(tc.tile_pool(name="keep", bufs=1))
         nat = ctx.enter_context(tc.tile_pool(name="nat", bufs=NAT_BUFS))
+        stg = ctx.enter_context(tc.tile_pool(name="stg", bufs=8))
         psum = ctx.enter_context(tc.psum_pool(name="psum", bufs=1))
 
         ident = const.tile([P, P], F32, name="ident")
@@ -43,17 +52,18 @@ def tile_ternarylinear_kernel(tc, x, weight, out):
         nc.vector.memset(ones_bf[:], 1.0)
         ones_f = const.tile([P, P], F32, name="ones_f")
         nc.vector.memset(ones_f[:], 1.0)
-        partv = const.tile([P, NCH], F32, name="partv")
+        partv = const.tile([P, 16], F32, name="partv")
+        nc.vector.memset(partv[:], 0.0)
         junk = const.tile([P, 512], F32, name="junk")
         nc.scalar.activation(out=junk[:, 0:1], in_=ones_f[:, 0:1], func=ACT.Copy)
         tsum = const.tile([P, 1], F32, name="tsum")
         vsum = const.tile([P, 1], F32, name="vsum")
         mean = const.tile([P, 1], F32, name="mean")
 
-        raw = [keep.tile([P, 4096], F32, name="raw%d" % b, align_bytes=64) for b in range(NOB)]
-        mag = [keep.tile([P, 4096], F32, name="mag%d" % b, align_bytes=64) for b in range(NOB)]
-        wcod = [keep.tile([P, 2048], U32, name="wcod%d" % b, align_bytes=64) for b in range(NOB)]
-        wpl = [keep.tile([P, 2048], U8, name="wpl%d" % b, align_bytes=64) for b in range(NOB)]
+        raw = [keep.tile([P, 8 * width[b]], F32, name="raw%d" % b, align_bytes=64) for b in range(nb)]
+        mag = [keep.tile([P, 8 * width[b]], F32, name="mag%d" % b, align_bytes=64) for b in range(nb)]
+        wcod = [keep.tile([P, NG * width[b]], U32, name="wcod%d" % b, align_bytes=64) for b in range(nb)]
+        wpl = [keep.tile([P, NG * width[b]], U8, name="wpl%d" % b, align_bytes=64) for b in range(nb)]
         xcod = [keep.tile([P, 512], U32, name="xcod%d" % i, align_bytes=64) for i in range(NI)]
         xpl = [keep.tile([P, 512], U8, name="xpl%d" % i, align_bytes=64) for i in range(NI)]
         banks = [psum.tile([P, 512], F32, name="bank%d" % b) for b in range(8)]
@@ -77,179 +87,170 @@ def tile_ternarylinear_kernel(tc, x, weight, out):
                     in_=banks[pair[h]][:].rearrange("p (g u o) -> p g o u", g=2, u=2),
                 )
 
-        def chunk_view(tile_ap, dtype, c4, per_col):
-            return tile_ap[:].bitcast(dtype).rearrange("p (g e) -> p g e", g=NG)[
-                :, :, c4 * P * per_col : (c4 + 1) * P * per_col
-            ]
+        steps = []
+        b = 0
+        while b < nb:
+            if BLOCK_CHUNKS[b] == 1:
+                steps.append((b, 0))
+                b += 1
+            else:
+                steps.extend([(b, 0), (b + 1, 0), (b, 1), (b + 1, 1)])
+                b += 2
 
-        wn = {}
-        xn = {}
-        for c in range(NAT_BUFS):
-            wn[c] = load(weight[c * P : (c + 1) * P, :])
+        def rows_of(s):
+            if s < NCH:
+                c = first[steps[s][0]] + steps[s][1]
+                return weight[c * P : (c + 1) * P, :]
+            return x[(s - NCH) * P : (s - NCH + 1) * P, :]
+
+        tiles = {}
+        for s in range(NAT_BUFS):
+            tiles[s] = load(rows_of(s))
         n_tmm = T_SLICES * NCH
         tmm = [0]
 
-        def tensor_sum(c):
-            ob, c4 = c // 4, c % 4
+        def part_view(tile_ap, dtype, s, per_col):
+            cc = steps[s][1]
+            return tile_ap[:].bitcast(dtype).rearrange("p (g e) -> p g e", g=NG)[
+                :, :, cc * P * per_col : (cc + 1) * P * per_col
+            ]
+
+        def magnitude(s):
+            b = steps[s][0]
+            nc.vector.tensor_scalar(
+                out=part_view(mag[b], I32, s, 2),
+                in0=part_view(raw[b], I32, s, 2),
+                scalar1=MAG_BITS,
+                scalar2=None,
+                op0=ALU.bitwise_and,
+            )
+
+        def tensor_sum(s):
+            b, cc = steps[s]
             for g in range(T_SLICES):
+                a = g * 4 * width[b] + cc * 512
                 nc.tensor.matmul(
                     out=banks[6][:],
                     lhsT=ones_bf[:],
-                    rhs=mag[ob][:].bitcast(BF16)[:, g * 2048 + c4 * 512 : g * 2048 + (c4 + 1) * 512],
+                    rhs=mag[b][:].bitcast(BF16)[:, a : a + 512],
                     start=(tmm[0] == 0),
                     stop=(tmm[0] == n_tmm - 1),
                 )
                 tmm[0] += 1
 
-        def vector_sum(c):
-            part = chunk_view(mag[c // 4], BF16, c % 4, 4)[:, T_SLICES:NG, :]
+        def vector_sum(s):
+            part = part_view(mag[steps[s][0]], BF16, s, 4)[:, T_SLICES:NG, :]
             nc.vector.tensor_scalar(
-                out=part, in0=part, scalar1=1.0, scalar2=None, op0=ALU.mult, op1=ALU.add, accum_out=partv[:, c : c + 1]
+                out=part, in0=part, scalar1=1.0, scalar2=None, op0=ALU.mult, op1=ALU.add, accum_out=partv[:, s : s + 1]
             )
 
-        def half_sign(c):
-            v = chunk_view(raw[c // 4], BF16, c % 4, 4)
-            nc.vector.tensor_scalar(out=v, in0=v, scalar1=0.0, scalar2=0.5, op0=ALU.is_ge, op1=ALU.subtract)
-
-        for c in range(NCH):
-            ob, c4 = c // 4, c % 4
-            pair = ((2 * c) % TR_BANKS, (2 * c + 1) % TR_BANKS)
-            transposes(wn[c], pair)
-            if c >= 2:
-                tensor_sum(c - 2)
-            exits(raw[ob][:].rearrange("p (g o u) -> p g o u", g=NG, u=2)[:, :, c4 * P : (c4 + 1) * P, :], pair, nc.scalar.copy)
-            nc.vector.tensor_scalar(
-                out=chunk_view(mag[ob], I32, c4, 2),
-                in0=chunk_view(raw[ob], I32, c4, 2),
-                scalar1=MAG_BITS,
-                scalar2=None,
-                op0=ALU.bitwise_and,
+        for s in range(NCH):
+            b, cc = steps[s]
+            pair = ((2 * s) % TR_BANKS, (2 * s + 1) % TR_BANKS)
+            transposes(tiles[s], pair)
+            if s >= SUM_LAG:
+                tensor_sum(s - SUM_LAG)
+            exits(
+                raw[b][:].rearrange("p (g o u) -> p g o u", g=NG, u=2)[:, :, cc * P : (cc + 1) * P, :], pair, nc.scalar.copy
             )
-            if c >= 1:
-                vector_sum(c - 1)
-                half_sign(c - 1)
-            nxt = c + NAT_BUFS
-            if nxt < NCH:
-                wn[nxt] = load(weight[nxt * P : (nxt + 1) * P, :])
-            elif nxt < NCH + NI:
-                xn[nxt - NCH] = load(x[(nxt - NCH) * P : (nxt - NCH + 1) * P, :])
+            magnitude(s)
+            if s >= 1:
+                vector_sum(s - 1)
+            tiles[s + NAT_BUFS] = load(rows_of(s + NAT_BUFS))
 
         xg = {}
 
-        def x_turn(i):
-            x_transposes(i)
-            x_exits(i, nc.scalar.copy)
-
         def x_transposes(i):
-            transposes(xn[i], X_BANKS[i])
+            transposes(tiles[NCH + i], X_BANKS[i])
 
         def x_exits(i, copy):
             xg[i] = nat.tile([P, 1024], F32, name="xgt", tag="nat", align_bytes=64)
             exits(xg[i][:].rearrange("p (g o u) -> p g o u", g=NG, u=2), X_BANKS[i], copy)
 
+        def x_turn(i):
+            x_transposes(i)
+            x_exits(i, nc.scalar.copy)
+
         x_ready = []
-        t_ready = []
-        count = {}
-        nxt_j = [0] * NI
+        b_ready = []
+        n_group = [0]
 
-        def issue(last):
-            for i in x_ready:
-                top = len(t_ready) if (i < LEAD or last or len(t_ready) < NG) else len(t_ready) - 1
-                while nxt_j[i] < top:
-                    one_pass(nxt_j[i], i)
-                    nxt_j[i] += 1
-
-        def leave(b, i, copy):
-            ob, o0, w = BLOCKS[b]
-            st = nat.tile([P, 512], F32, name="stage", tag="nat", align_bytes=64)
-            copy(out=st[:, 0:w], in_=banks[i][:, 0:w])
-            nc.sync.dma_start(out=out[i * P : (i + 1) * P, ob * 512 + o0 : ob * 512 + o0 + w], in_=st[:, 0:w])
-
-        def one_pass(j, i):
-            b, g = j // NG, j % NG
-            ob, o0, w = BLOCKS[b]
-            n = count.get((b, i), 0)
-            nc.tensor.matmul_mx(
-                out=banks[i][:, 0:w],
-                lhsT=xcod[i][:, g * P : (g + 1) * P].bitcast(FP8X4),
-                lhsT_scale=xpl[i][:, g * P : (g + 1) * P],
-                rhs=wcod[ob][:, g * 512 + o0 : g * 512 + o0 + w].bitcast(FP8X4),
-                rhs_scale=wpl[ob][:, g * 512 + o0 : g * 512 + o0 + w],
-                start=(n == 0),
-                stop=(n == NG - 1),
-            )
-            count[(b, i)] = n + 1
-            if n == NG - 1:
-                if b == len(BLOCKS) - 1 and i % 2 == 1:
-                    leave(b, i, nc.vector.tensor_copy)
-                else:
-                    leave(b, i, nc.scalar.copy)
+        def group(b, i):
+            w = width[b]
+            bank = banks[MX_BANKS[n_group[0] % len(MX_BANKS)]]
+            for g in range(NG):
+                nc.tensor.matmul_mx(
+                    out=bank[:, 0:w],
+                    lhsT=xcod[i][:, g * P : (g + 1) * P].bitcast(FP8X4),
+                    lhsT_scale=xpl[i][:, g * P : (g + 1) * P],
+                    rhs=wcod[b][:, g * w : (g + 1) * w].bitcast(FP8X4),
+                    rhs_scale=wpl[b][:, g * w : (g + 1) * w],
+                    start=(g == 0),
+                    stop=(g == NG - 1),
+                )
+            st = stg.tile([P, 256], F32, name="stage")
+            if b == nb - 1 and i % 2 == 1:
+                nc.vector.tensor_copy(out=st[:, 0:w], in_=bank[:, 0:w])
+            else:
+                nc.scalar.copy(out=st[:, 0:w], in_=bank[:, 0:w])
+            nc.sync.dma_start(out=out[i * P : (i + 1) * P, first[b] * P : first[b] * P + w], in_=st[:, 0:w])
+            n_group[0] += 1
 
         def x_quant(i):
             nc.vector.quantize_mx(out=xcod[i][:].bitcast(FP8X4), scales=xpl[i][:], in_=xg[i][:].bitcast(BF16))
             x_ready.append(i)
-            issue(False)
+            for b in b_ready:
+                group(b, i)
 
-        def mask(j):
-            ob, o0, w = BLOCKS[j // NG]
-            a = (j % NG) * 2048 + 4 * o0
-            v = mag[ob][:].bitcast(BF16)[:, a : a + 4 * w]
-            nc.vector.tensor_scalar(out=v, in0=v, scalar1=mean[:, 0:1], scalar2=2.0, op0=ALU.is_gt, op1=ALU.mult)
+        def mask(b):
+            v = mag[b][:].bitcast(BF16)
+            nc.vector.tensor_scalar(out=v, in0=v, scalar1=mean[:, 0:1], scalar2=None, op0=ALU.is_gt)
 
-        def merge(j):
-            ob, o0, w = BLOCKS[j // NG]
-            a = (j % NG) * 2048 + 4 * o0
-            r = raw[ob][:].bitcast(BF16)[:, a : a + 4 * w]
-            nc.vector.tensor_tensor(out=r, in0=mag[ob][:].bitcast(BF16)[:, a : a + 4 * w], in1=r, op=ALU.mult)
-
-        def t_quant(j):
-            ob, o0, w = BLOCKS[j // NG]
-            g = j % NG
-            nc.vector.quantize_mx(
-                out=wcod[ob][:, g * 512 + o0 : g * 512 + o0 + w].bitcast(FP8X4),
-                scales=wpl[ob][:, g * 512 + o0 : g * 512 + o0 + w],
-                in_=raw[ob][:].bitcast(BF16)[:, g * 2048 + 4 * o0 : g * 2048 + 4 * (o0 + w)],
+        def merge(b):
+            r = raw[b][:].bitcast(I32)
+            nc.vector.scalar_tensor_tensor(
+                out=r, in0=r, scalar=SIGN_BITS, in1=mag[b][:].bitcast(I32), op0=ALU.bitwise_and, op1=ALU.bitwise_or
             )
-            t_ready.append(j)
-            issue(j == len(BLOCKS) * NG - 1)
+
+        def t_quant(b):
+            nc.vector.quantize_mx(out=wcod[b][:].bitcast(FP8X4), scales=wpl[b][:], in_=raw[b][:].bitcast(BF16))
+            b_ready.append(b)
+            for i in x_ready:
+                group(b, i)
 
         tensor_sum(NCH - 2)
         x_transposes(0)
         vector_sum(NCH - 1)
         tensor_sum(NCH - 1)
         nc.scalar.activation(out=junk[:], in_=banks[6][:], func=ACT.Copy, accum_out=tsum[:])
+        x_exits(0, nc.scalar.copy)
         x_turn(1)
-        x_exits(0, nc.vector.tensor_copy)
-        nc.tensor.matmul(out=banks[7][:, 0:NCH], lhsT=ones_f[:], rhs=partv[:], start=True, stop=True)
-        nc.vector.tensor_reduce(out=vsum[:], in_=banks[7][:, 0:NCH], axis=AX.X, op=ALU.add)
+        nc.tensor.matmul(out=banks[7][:, 0:16], lhsT=ones_f[:], rhs=partv[:], start=True, stop=True)
+        nc.vector.tensor_reduce(out=vsum[:], in_=banks[7][:, 0:16], axis=AX.X, op=ALU.add)
         nc.vector.tensor_scalar(
             out=mean[:], in0=vsum[:], scalar1=tsum[:, 0:1], scalar2=1.0 / (OUTF * K), op0=ALU.add, op1=ALU.mult
         )
-        for i in range(2, 7):
+        for i in range(2, 6):
             x_turn(i)
-        half_sign(NCH - 1)
-        nj = len(BLOCKS) * NG
         mask(0)
         x_quant(0)
         merge(0)
         x_quant(1)
         t_quant(0)
         x_quant(2)
+        x_turn(6)
         x_quant(3)
         x_turn(7)
         mask(1)
         x_quant(4)
         merge(1)
         x_quant(5)
+        mask(2)
         t_quant(1)
         x_quant(6)
-        mask(2)
         x_quant(7)
-        merge(2)
-        mask(3)
-        t_quant(2)
-        for j in range(3, nj):
-            merge(j)
-            if j + 1 < nj:
-                mask(j + 1)
-            t_quant(j)
+        for b in range(2, nb):
+            merge(b)
+            if b + 1 < nb:
+                mask(b + 1)
+            t_quant(b)

@@ -10,7 +10,6 @@ U32 = mybir.dt.uint32
 U8 = mybir.dt.uint8
 FP8X4 = mybir.dt.float8_e4m3fn_x4
 ALU = mybir.AluOpType
-AX = mybir.AxisListType
 ACT = mybir.ActivationFunctionType
 
 P = 128
@@ -20,15 +19,17 @@ NG = K // 512
 NI = TOKENS // P
 NCH = OUTF // P
 MAG_BITS = 0x7FFF7FFF
-SIGN_BITS = -2147450880
-MANUAL = True
-NAT_BUFS = 8
+TOP_BITS = -1073692672
+UPPER_HALF = -65536
+HALF_STEP = 32768
+JUST_UNDER_TWO = 2.0 - 2.0**-8
+NAT_BUFS = 12
 TR_BANKS = 6
-BLOCK_CHUNKS = (1, 1, 2, 2, 2, 2, 2, 2, 1, 1)
-T_SLICES = 2
-SUM_LAG = 2
+NCOL = 8
+BLOCK_CHUNKS = (1, 1, 2, 2, 2, 2, 2, 2, 2)
+VECTOR_EXITS = (4, 8, 12)
 MX_BANKS = (0, 1, 2, 3)
-X_BANKS = ((2, 3), (4, 5), (0, 1), (6, 7), (4, 5), (6, 7), (4, 5), (6, 7))
+X_BANKS = ((2, 3), (4, 5), (6, 7), (4, 5), (6, 7), (4, 5), (6, 7), (4, 5))
 
 
 def tile_ternarylinear_kernel(tc, x, weight, out):
@@ -36,42 +37,59 @@ def tile_ternarylinear_kernel(tc, x, weight, out):
     nb = len(BLOCK_CHUNKS)
     first = [sum(BLOCK_CHUNKS[:b]) for b in range(nb)]
     width = [P * n for n in BLOCK_CHUNKS]
-    block_of = [b for b in range(nb) for q in range(BLOCK_CHUNKS[b])]
     with ExitStack() as ctx:
-        if MANUAL:
-            ctx.enter_context(tc.manual_schedule())
+        ctx.enter_context(tc.manual_schedule())
         const = ctx.enter_context(tc.tile_pool(name="const", bufs=1))
         keep = ctx.enter_context(tc.tile_pool(name="keep", bufs=1))
         nat = ctx.enter_context(tc.tile_pool(name="nat", bufs=NAT_BUFS))
+        mags = ctx.enter_context(tc.tile_pool(name="mags", bufs=3))
+        xgs = ctx.enter_context(tc.tile_pool(name="xgs", bufs=3))
         stg = ctx.enter_context(tc.tile_pool(name="stg", bufs=8))
         psum = ctx.enter_context(tc.psum_pool(name="psum", bufs=1))
 
         ident = const.tile([P, P], F32, name="ident")
         make_identity(nc, ident[:])
-        ones_bf = const.tile([P, P], BF16, name="ones_bf")
+        ones_bf = const.tile([P, NCOL], BF16, name="ones_bf")
         nc.vector.memset(ones_bf[:], 1.0)
         ones_f = const.tile([P, P], F32, name="ones_f")
         nc.vector.memset(ones_f[:], 1.0)
-        partv = const.tile([P, 16], F32, name="partv")
-        nc.vector.memset(partv[:], 0.0)
-        junk = const.tile([P, 512], F32, name="junk")
-        nc.scalar.activation(out=junk[:, 0:1], in_=ones_f[:, 0:1], func=ACT.Copy)
-        tsum = const.tile([P, 1], F32, name="tsum")
-        vsum = const.tile([P, 1], F32, name="vsum")
-        mean = const.tile([P, 1], F32, name="mean")
+        junk = const.tile([P, 1], F32, name="junk")
+        nc.scalar.activation(out=junk[:], in_=ones_f[:, 0:1], func=ACT.Copy)
+        tsum = const.tile([P, NCOL], F32, name="tsum")
+        thr = const.tile([P, 1], F32, name="thr")
+        inv = const.tile([P, 1], F32, name="inv")
 
         raw = [keep.tile([P, 8 * width[b]], F32, name="raw%d" % b, align_bytes=64) for b in range(nb)]
-        mag = [keep.tile([P, 8 * width[b]], F32, name="mag%d" % b, align_bytes=64) for b in range(nb)]
         wcod = [keep.tile([P, NG * width[b]], U32, name="wcod%d" % b, align_bytes=64) for b in range(nb)]
         wpl = [keep.tile([P, NG * width[b]], U8, name="wpl%d" % b, align_bytes=64) for b in range(nb)]
         xcod = [keep.tile([P, 512], U32, name="xcod%d" % i, align_bytes=64) for i in range(NI)]
         xpl = [keep.tile([P, 512], U8, name="xpl%d" % i, align_bytes=64) for i in range(NI)]
         banks = [psum.tile([P, 512], F32, name="bank%d" % b) for b in range(8)]
 
-        def load(rows):
-            t = nat.tile([P, K], BF16, name="natt", tag="nat", align_bytes=64)
-            nc.sync.dma_start(out=t[:], in_=rows)
-            return t
+        steps = []
+        b = 0
+        while b < nb:
+            if BLOCK_CHUNKS[b] == 1:
+                steps.append((b, 0))
+                b += 1
+            elif b + 1 < nb:
+                steps.extend([(b, 0), (b + 1, 0), (b, 1), (b + 1, 1)])
+                b += 2
+            else:
+                steps.extend([(b, 0), (b, 1)])
+                b += 1
+
+        def rows_of(s):
+            if s < NCH:
+                c = first[steps[s][0]] + steps[s][1]
+                return weight[c * P : (c + 1) * P, :]
+            return x[(s - NCH) * P : (s - NCH + 1) * P, :]
+
+        tiles = {}
+
+        def load(s):
+            tiles[s] = nat.tile([P, K], BF16, name="natt", tag="nat", align_bytes=64)
+            nc.sync.dma_start(out=tiles[s][:], in_=rows_of(s))
 
         def transposes(src, pair):
             words = src[:].bitcast(F32)
@@ -87,93 +105,67 @@ def tile_ternarylinear_kernel(tc, x, weight, out):
                     in_=banks[pair[h]][:].rearrange("p (g u o) -> p g o u", g=2, u=2),
                 )
 
-        steps = []
-        b = 0
-        while b < nb:
-            if BLOCK_CHUNKS[b] == 1:
-                steps.append((b, 0))
-                b += 1
-            else:
-                steps.extend([(b, 0), (b + 1, 0), (b, 1), (b + 1, 1)])
-                b += 2
-
-        def rows_of(s):
-            if s < NCH:
-                c = first[steps[s][0]] + steps[s][1]
-                return weight[c * P : (c + 1) * P, :]
-            return x[(s - NCH) * P : (s - NCH + 1) * P, :]
-
-        tiles = {}
-        for s in range(NAT_BUFS):
-            tiles[s] = load(rows_of(s))
-        n_tmm = T_SLICES * NCH
-        tmm = [0]
-
-        def part_view(tile_ap, dtype, s, per_col):
-            cc = steps[s][1]
-            return tile_ap[:].bitcast(dtype).rearrange("p (g e) -> p g e", g=NG)[
-                :, :, cc * P * per_col : (cc + 1) * P * per_col
-            ]
+        magn = {}
 
         def magnitude(s):
-            b = steps[s][0]
+            magn[s] = mags.tile([P, K], BF16, name="magt", tag="mag", align_bytes=64)
             nc.vector.tensor_scalar(
-                out=part_view(mag[b], I32, s, 2),
-                in0=part_view(raw[b], I32, s, 2),
+                out=magn[s][:].bitcast(I32),
+                in0=tiles[s][:].bitcast(I32),
                 scalar1=MAG_BITS,
                 scalar2=None,
                 op0=ALU.bitwise_and,
             )
 
-        def tensor_sum(s):
-            b, cc = steps[s]
-            for g in range(T_SLICES):
-                a = g * 4 * width[b] + cc * 512
+        def sums(s):
+            for j in range(K // P):
                 nc.tensor.matmul(
-                    out=banks[6][:],
-                    lhsT=ones_bf[:],
-                    rhs=mag[b][:].bitcast(BF16)[:, a : a + 512],
-                    start=(tmm[0] == 0),
-                    stop=(tmm[0] == n_tmm - 1),
+                    out=banks[7][:, 0:NCOL],
+                    lhsT=magn[s][:, j * P : (j + 1) * P],
+                    rhs=ones_bf[:],
+                    start=(s == 0 and j == 0),
+                    stop=(s == NCH - 1 and j == K // P - 1),
                 )
-                tmm[0] += 1
 
-        def vector_sum(s):
-            part = part_view(mag[steps[s][0]], BF16, s, 4)[:, T_SLICES:NG, :]
-            nc.vector.tensor_scalar(
-                out=part, in0=part, scalar1=1.0, scalar2=None, op0=ALU.mult, op1=ALU.add, accum_out=partv[:, s : s + 1]
-            )
-
+        for s in range(NAT_BUFS):
+            load(s)
         for s in range(NCH):
             b, cc = steps[s]
             pair = ((2 * s) % TR_BANKS, (2 * s + 1) % TR_BANKS)
             transposes(tiles[s], pair)
-            if s >= SUM_LAG:
-                tensor_sum(s - SUM_LAG)
-            exits(
-                raw[b][:].rearrange("p (g o u) -> p g o u", g=NG, u=2)[:, :, cc * P : (cc + 1) * P, :], pair, nc.scalar.copy
-            )
             magnitude(s)
             if s >= 1:
-                vector_sum(s - 1)
-            tiles[s + NAT_BUFS] = load(rows_of(s + NAT_BUFS))
+                sums(s - 1)
+            exits(
+                raw[b][:].rearrange("p (g o u) -> p g o u", g=NG, u=2)[:, :, cc * P : (cc + 1) * P, :],
+                pair,
+                nc.vector.tensor_copy if s in VECTOR_EXITS else nc.scalar.copy,
+            )
+            if s + NAT_BUFS < NCH + NI:
+                load(s + NAT_BUFS)
+        sums(NCH - 1)
+        nc.vector.tensor_copy(out=tsum[:], in_=banks[7][:, 0:NCOL])
+        nc.tensor.matmul(out=banks[6][:, 0:NCOL], lhsT=ones_f[:], rhs=tsum[:], start=True, stop=True)
+        nc.vector.tensor_scalar(out=thr[:], in0=banks[6][:, 0:1], scalar1=2.0**-100, scalar2=None, op0=ALU.max)
+        nc.vector.tensor_scalar(
+            out=thr[:].bitcast(I32),
+            in0=thr[:].bitcast(I32),
+            scalar1=UPPER_HALF,
+            scalar2=HALF_STEP,
+            op0=ALU.bitwise_and,
+            op1=ALU.bitwise_or,
+        )
+        nc.vector.reciprocal(out=inv[:], in_=thr[:])
 
         xg = {}
-
-        def x_transposes(i):
-            transposes(tiles[NCH + i], X_BANKS[i])
-
-        def x_exits(i, copy):
-            xg[i] = nat.tile([P, 1024], F32, name="xgt", tag="nat", align_bytes=64)
-            exits(xg[i][:].rearrange("p (g o u) -> p g o u", g=NG, u=2), X_BANKS[i], copy)
-
-        def x_turn(i):
-            x_transposes(i)
-            x_exits(i, nc.scalar.copy)
-
         x_ready = []
         b_ready = []
         n_group = [0]
+
+        def x_turn(i):
+            transposes(tiles[NCH + i], X_BANKS[i])
+            xg[i] = xgs.tile([P, 1024], F32, name="xgt", tag="xg", align_bytes=64)
+            exits(xg[i][:].rearrange("p (g o u) -> p g o u", g=NG, u=2), X_BANKS[i], nc.scalar.copy)
 
         def group(b, i):
             w = width[b]
@@ -190,9 +182,9 @@ def tile_ternarylinear_kernel(tc, x, weight, out):
                 )
             st = stg.tile([P, 256], F32, name="stage")
             if b == nb - 1 and i % 2 == 1:
-                nc.vector.tensor_copy(out=st[:, 0:w], in_=bank[:, 0:w])
+                nc.vector.tensor_scalar(out=st[:, 0:w], in0=bank[:, 0:w], scalar1=0.5, scalar2=None, op0=ALU.mult)
             else:
-                nc.scalar.copy(out=st[:, 0:w], in_=bank[:, 0:w])
+                nc.scalar.activation(out=st[:, 0:w], in_=bank[:, 0:w], func=ACT.Copy, scale=0.5)
             nc.sync.dma_start(out=out[i * P : (i + 1) * P, first[b] * P : first[b] * P + w], in_=st[:, 0:w])
             n_group[0] += 1
 
@@ -202,15 +194,15 @@ def tile_ternarylinear_kernel(tc, x, weight, out):
             for b in b_ready:
                 group(b, i)
 
-        def mask(b):
-            v = mag[b][:].bitcast(BF16)
-            nc.vector.tensor_scalar(out=v, in0=v, scalar1=mean[:, 0:1], scalar2=None, op0=ALU.is_gt)
-
-        def merge(b):
-            r = raw[b][:].bitcast(I32)
-            nc.vector.scalar_tensor_tensor(
-                out=r, in0=r, scalar=SIGN_BITS, in1=mag[b][:].bitcast(I32), op0=ALU.bitwise_and, op1=ALU.bitwise_or
+        def scale(b):
+            v = raw[b][:].bitcast(BF16)
+            nc.vector.tensor_scalar(
+                out=v, in0=v, scalar1=inv[:], scalar2=JUST_UNDER_TWO * (OUTF * K), op0=ALU.mult, op1=ALU.mult
             )
+
+        def cut(b):
+            r = raw[b][:].bitcast(I32)
+            nc.vector.tensor_scalar(out=r, in0=r, scalar1=TOP_BITS, scalar2=None, op0=ALU.bitwise_and)
 
         def t_quant(b):
             nc.vector.quantize_mx(out=wcod[b][:].bitcast(FP8X4), scales=wpl[b][:], in_=raw[b][:].bitcast(BF16))
@@ -218,39 +210,37 @@ def tile_ternarylinear_kernel(tc, x, weight, out):
             for i in x_ready:
                 group(b, i)
 
-        tensor_sum(NCH - 2)
-        x_transposes(0)
-        vector_sum(NCH - 1)
-        tensor_sum(NCH - 1)
-        nc.scalar.activation(out=junk[:], in_=banks[6][:], func=ACT.Copy, accum_out=tsum[:])
-        x_exits(0, nc.scalar.copy)
+        x_turn(0)
+        scale(0)
+        cut(0)
         x_turn(1)
-        nc.tensor.matmul(out=banks[7][:, 0:16], lhsT=ones_f[:], rhs=partv[:], start=True, stop=True)
-        nc.vector.tensor_reduce(out=vsum[:], in_=banks[7][:, 0:16], axis=AX.X, op=ALU.add)
-        nc.vector.tensor_scalar(
-            out=mean[:], in0=vsum[:], scalar1=tsum[:, 0:1], scalar2=1.0 / (OUTF * K), op0=ALU.add, op1=ALU.mult
-        )
-        for i in range(2, 6):
-            x_turn(i)
-        mask(0)
         x_quant(0)
-        merge(0)
-        x_quant(1)
+        x_turn(2)
         t_quant(0)
+        scale(1)
+        x_quant(1)
+        x_turn(3)
+        cut(1)
         x_quant(2)
-        x_turn(6)
-        x_quant(3)
-        x_turn(7)
-        mask(1)
-        x_quant(4)
-        merge(1)
-        x_quant(5)
-        mask(2)
+        x_turn(4)
         t_quant(1)
+        scale(2)
+        x_quant(3)
+        x_turn(5)
+        cut(2)
+        x_quant(4)
+        x_turn(6)
+        t_quant(2)
+        scale(3)
+        x_quant(5)
+        x_turn(7)
+        cut(3)
         x_quant(6)
+        t_quant(3)
+        scale(4)
         x_quant(7)
-        for b in range(2, nb):
-            merge(b)
+        for b in range(4, nb):
+            cut(b)
             if b + 1 < nb:
-                mask(b + 1)
+                scale(b + 1)
             t_quant(b)

@@ -25,7 +25,7 @@ HALF_STEP = 32768
 JUST_UNDER_TWO = 2.0 - 2.0**-8
 NAT_BUFS = 12
 TR_BANKS = 6
-NCOL = 8
+NCOL = 48
 BLOCK_CHUNKS = (1, 1, 2, 2, 2, 2, 2, 2, 2)
 VECTOR_EXITS = (4, 8, 12)
 MX_BANKS = (0, 1, 2, 3)

@@ -24,12 +24,13 @@ UPPER_HALF = -65536
 HALF_STEP = 32768
 JUST_UNDER_TWO = 2.0 - 2.0**-8
 NAT_BUFS = 12
-TR_BANKS = 6
+FIRST_PIECES = 4
 NCOL = 48
 BLOCK_CHUNKS = (1, 1, 2, 2, 2, 2, 2, 2, 2)
-VECTOR_EXITS = (4, 8, 12)
-MX_BANKS = (0, 1, 2, 3)
-X_BANKS = ((2, 3), (4, 5), (6, 7), (4, 5), (6, 7), (4, 5), (6, 7), (4, 5))
+VECTOR_SUMS = (2, 6, 10)
+PAIRS = ((0, 1), (2, 3), (4, 5))
+LATE_PAIRS = ((2, 3), (6, 7), (4, 5))
+X_GROUPS = 10
 
 
 def tile_ternarylinear_kernel(tc, x, weight, out):
@@ -55,7 +56,8 @@ def tile_ternarylinear_kernel(tc, x, weight, out):
         nc.vector.memset(ones_f[:], 1.0)
         junk = const.tile([P, 1], F32, name="junk")
         nc.scalar.activation(out=junk[:], in_=ones_f[:, 0:1], func=ACT.Copy)
-        tsum = const.tile([P, NCOL], F32, name="tsum")
+        tsum = const.tile([P, 1], F32, name="tsum")
+        vsum = const.tile([P, len(VECTOR_SUMS)], F32, name="vsum")
         thr = const.tile([P, 1], F32, name="thr")
         inv = const.tile([P, 1], F32, name="inv")
 
@@ -89,7 +91,10 @@ def tile_ternarylinear_kernel(tc, x, weight, out):
 
         def load(s):
             tiles[s] = nat.tile([P, K], BF16, name="natt", tag="nat", align_bytes=64)
-            nc.sync.dma_start(out=tiles[s][:], in_=rows_of(s))
+            pieces = FIRST_PIECES if s == 0 else 1
+            for j in range(pieces):
+                cols = slice(j * K // pieces, (j + 1) * K // pieces)
+                nc.sync.dma_start(out=tiles[s][:, cols], in_=rows_of(s)[:, cols])
 
         def transposes(src, pair):
             words = src[:].bitcast(F32)
@@ -118,6 +123,13 @@ def tile_ternarylinear_kernel(tc, x, weight, out):
             )
 
         def sums(s):
+            if s in VECTOR_SUMS:
+                j = VECTOR_SUMS.index(s)
+                nc.vector.tensor_scalar(
+                    out=magn[s][:], in0=magn[s][:], scalar1=1.0, scalar2=None, op0=ALU.mult, op1=ALU.add,
+                    accum_out=vsum[:, j : j + 1],
+                )
+                return
             for j in range(K // P):
                 nc.tensor.matmul(
                     out=banks[7][:, 0:NCOL],
@@ -129,23 +141,30 @@ def tile_ternarylinear_kernel(tc, x, weight, out):
 
         for s in range(NAT_BUFS):
             load(s)
-        for s in range(NCH):
+        def w_turn(s, pair):
             b, cc = steps[s]
-            pair = ((2 * s) % TR_BANKS, (2 * s + 1) % TR_BANKS)
             transposes(tiles[s], pair)
-            magnitude(s)
-            if s >= 1:
-                sums(s - 1)
             exits(
                 raw[b][:].rearrange("p (g o u) -> p g o u", g=NG, u=2)[:, :, cc * P : (cc + 1) * P, :],
                 pair,
-                nc.vector.tensor_copy if s in VECTOR_EXITS else nc.scalar.copy,
+                nc.scalar.copy,
             )
+
+        for s in range(NCH):
+            if s < NCH - 1:
+                w_turn(s, PAIRS[s % 3])
+            magnitude(s)
+            if s >= 1:
+                sums(s - 1)
             if s + NAT_BUFS < NCH + NI:
                 load(s + NAT_BUFS)
         sums(NCH - 1)
-        nc.vector.tensor_copy(out=tsum[:], in_=banks[7][:, 0:NCOL])
-        nc.tensor.matmul(out=banks[6][:, 0:NCOL], lhsT=ones_f[:], rhs=tsum[:], start=True, stop=True)
+        nc.vector.tensor_copy(out=tsum[:], in_=banks[7][:, 0:1])
+        parts = [vsum[:, j : j + 1] for j in range(len(VECTOR_SUMS))] + [tsum[:]]
+        for j, part in enumerate(parts):
+            nc.tensor.matmul(
+                out=banks[6][:, 0:1], lhsT=ones_f[:], rhs=part, start=(j == 0), stop=(j == len(parts) - 1)
+            )
         nc.vector.tensor_scalar(out=thr[:], in0=banks[6][:, 0:1], scalar1=2.0**-100, scalar2=None, op0=ALU.max)
         nc.vector.tensor_scalar(
             out=thr[:].bitcast(I32),
@@ -158,18 +177,21 @@ def tile_ternarylinear_kernel(tc, x, weight, out):
         nc.vector.reciprocal(out=inv[:], in_=thr[:])
 
         xg = {}
+        n_turn = [0]
         x_ready = []
         b_ready = []
         n_group = [0]
 
         def x_turn(i):
-            transposes(tiles[NCH + i], X_BANKS[i])
+            pair = LATE_PAIRS[n_turn[0] % 3]
+            n_turn[0] += 1
+            transposes(tiles[NCH + i], pair)
             xg[i] = xgs.tile([P, 1024], F32, name="xgt", tag="xg", align_bytes=64)
-            exits(xg[i][:].rearrange("p (g o u) -> p g o u", g=NG, u=2), X_BANKS[i], nc.scalar.copy)
+            exits(xg[i][:].rearrange("p (g o u) -> p g o u", g=NG, u=2), pair, nc.scalar.copy)
 
         def group(b, i):
             w = width[b]
-            bank = banks[MX_BANKS[n_group[0] % len(MX_BANKS)]]
+            bank = banks[n_group[0] % (2 if n_group[0] < X_GROUPS else 4)]
             for g in range(NG):
                 nc.tensor.matmul_mx(
                     out=bank[:, 0:w],
@@ -211,29 +233,31 @@ def tile_ternarylinear_kernel(tc, x, weight, out):
                 group(b, i)
 
         x_turn(0)
+        x_turn(1)
+        w_turn(NCH - 1, LATE_PAIRS[2])
+        n_turn[0] += 1
         scale(0)
         cut(0)
-        x_turn(1)
-        x_quant(0)
         x_turn(2)
+        x_quant(0)
         t_quant(0)
+        x_turn(3)
         scale(1)
         x_quant(1)
-        x_turn(3)
+        x_turn(4)
         cut(1)
         x_quant(2)
-        x_turn(4)
+        x_turn(5)
         t_quant(1)
         scale(2)
         x_quant(3)
-        x_turn(5)
+        x_turn(6)
         cut(2)
         x_quant(4)
-        x_turn(6)
+        x_turn(7)
         t_quant(2)
         scale(3)
         x_quant(5)
-        x_turn(7)
         cut(3)
         x_quant(6)
         t_quant(3)

@@ -27,7 +27,7 @@ NAT_BUFS = 12
 FIRST_PIECES = 4
 NCOL = 48
 BLOCK_CHUNKS = (1, 1, 2, 2, 2, 2, 2, 2, 2)
-VECTOR_SUMS = (2, 6, 10)
+HEAD_WARM = 5
 PAIRS = ((0, 1), (2, 3), (4, 5))
 LATE_PAIRS = ((2, 3), (6, 7), (4, 5))
 X_GROUPS = 10
@@ -50,14 +50,13 @@ def tile_ternarylinear_kernel(tc, x, weight, out):
 
         ident = const.tile([P, P], F32, name="ident")
         make_identity(nc, ident[:])
-        ones_bf = const.tile([P, NCOL], BF16, name="ones_bf")
+        ones_bf = const.tile([P, 512], BF16, name="ones_bf", align_bytes=64)
         nc.vector.memset(ones_bf[:], 1.0)
         ones_f = const.tile([P, P], F32, name="ones_f")
         nc.vector.memset(ones_f[:], 1.0)
         junk = const.tile([P, 1], F32, name="junk")
         nc.scalar.activation(out=junk[:], in_=ones_f[:, 0:1], func=ACT.Copy)
         tsum = const.tile([P, 1], F32, name="tsum")
-        vsum = const.tile([P, len(VECTOR_SUMS)], F32, name="vsum")
         thr = const.tile([P, 1], F32, name="thr")
         inv = const.tile([P, 1], F32, name="inv")
 
@@ -123,22 +122,20 @@ def tile_ternarylinear_kernel(tc, x, weight, out):
             )
 
         def sums(s):
-            if s in VECTOR_SUMS:
-                j = VECTOR_SUMS.index(s)
-                nc.vector.tensor_scalar(
-                    out=magn[s][:], in0=magn[s][:], scalar1=1.0, scalar2=None, op0=ALU.mult, op1=ALU.add,
-                    accum_out=vsum[:, j : j + 1],
-                )
-                return
             for j in range(K // P):
                 nc.tensor.matmul(
                     out=banks[7][:, 0:NCOL],
                     lhsT=magn[s][:, j * P : (j + 1) * P],
-                    rhs=ones_bf[:],
+                    rhs=ones_bf[:, 0:NCOL],
                     start=(s == 0 and j == 0),
                     stop=(s == NCH - 1 and j == K // P - 1),
                 )
 
+        def warm(n):
+            for j in range(n):
+                nc.tensor.matmul(out=banks[1][:], lhsT=ones_bf[:, 0:P], rhs=ones_bf[:], start=True, stop=True)
+
+        warm(HEAD_WARM)
         for s in range(NAT_BUFS):
             load(s)
         def w_turn(s, pair):
@@ -160,11 +157,7 @@ def tile_ternarylinear_kernel(tc, x, weight, out):
                 load(s + NAT_BUFS)
         sums(NCH - 1)
         nc.vector.tensor_copy(out=tsum[:], in_=banks[7][:, 0:1])
-        parts = [vsum[:, j : j + 1] for j in range(len(VECTOR_SUMS))] + [tsum[:]]
-        for j, part in enumerate(parts):
-            nc.tensor.matmul(
-                out=banks[6][:, 0:1], lhsT=ones_f[:], rhs=part, start=(j == 0), stop=(j == len(parts) - 1)
-            )
+        nc.tensor.matmul(out=banks[6][:, 0:1], lhsT=ones_f[:], rhs=tsum[:], start=True, stop=True)
         nc.vector.tensor_scalar(out=thr[:], in0=banks[6][:, 0:1], scalar1=2.0**-100, scalar2=None, op0=ALU.max)
         nc.vector.tensor_scalar(
             out=thr[:].bitcast(I32),
@@ -232,13 +225,18 @@ def tile_ternarylinear_kernel(tc, x, weight, out):
             for i in x_ready:
                 group(b, i)
 
+        warm(1)
         x_turn(0)
+        warm(1)
         x_turn(1)
+        warm(1)
         w_turn(NCH - 1, LATE_PAIRS[2])
         n_turn[0] += 1
+        warm(1)
         scale(0)
         cut(0)
         x_turn(2)
+        warm(1)
         x_quant(0)
         t_quant(0)
         x_turn(3)

@@ -10,6 +10,7 @@ U32 = mybir.dt.uint32
 U8 = mybir.dt.uint8
 FP8X4 = mybir.dt.float8_e4m3fn_x4
 ALU = mybir.AluOpType
+AX = mybir.AxisListType
 ACT = mybir.ActivationFunctionType
 
 P = 128
@@ -25,9 +26,10 @@ HALF_STEP = 32768
 JUST_UNDER_TWO = 2.0 - 2.0**-8
 NAT_BUFS = 12
 FIRST_PIECES = 4
-NCOL = 48
+NCOL = 56
 BLOCK_CHUNKS = (1, 1, 2, 2, 2, 2, 2, 2, 2)
-HEAD_WARM = 5
+V_SLICE = 512
+HEAD_WARM = 2
 PAIRS = ((0, 1), (2, 3), (4, 5))
 LATE_PAIRS = ((2, 3), (6, 7), (4, 5))
 X_GROUPS = 10
@@ -57,6 +59,8 @@ def tile_ternarylinear_kernel(tc, x, weight, out):
         junk = const.tile([P, 1], F32, name="junk")
         nc.scalar.activation(out=junk[:], in_=ones_f[:, 0:1], func=ACT.Copy)
         tsum = const.tile([P, 1], F32, name="tsum")
+        vsums = const.tile([P, NCH], F32, name="vsums")
+        vsum = const.tile([P, 1], F32, name="vsum")
         thr = const.tile([P, 1], F32, name="thr")
         inv = const.tile([P, 1], F32, name="inv")
 
@@ -121,14 +125,20 @@ def tile_ternarylinear_kernel(tc, x, weight, out):
                 op0=ALU.bitwise_and,
             )
 
+        def vector_sum(s):
+            part = magn[s][:, K - V_SLICE : K]
+            nc.vector.tensor_scalar(
+                out=part, in0=part, scalar1=1.0, scalar2=None, op0=ALU.mult, op1=ALU.add, accum_out=vsums[:, s : s + 1]
+            )
+
         def sums(s):
-            for j in range(K // P):
+            for j in range((K - V_SLICE) // P):
                 nc.tensor.matmul(
                     out=banks[7][:, 0:NCOL],
                     lhsT=magn[s][:, j * P : (j + 1) * P],
                     rhs=ones_bf[:, 0:NCOL],
                     start=(s == 0 and j == 0),
-                    stop=(s == NCH - 1 and j == K // P - 1),
+                    stop=(s == NCH - 1 and j == (K - V_SLICE) // P - 1),
                 )
 
         def warm(n):
@@ -152,11 +162,14 @@ def tile_ternarylinear_kernel(tc, x, weight, out):
                 w_turn(s, PAIRS[s % 3])
             magnitude(s)
             if s >= 1:
+                vector_sum(s - 1)
                 sums(s - 1)
             if s + NAT_BUFS < NCH + NI:
                 load(s + NAT_BUFS)
+        vector_sum(NCH - 1)
+        nc.vector.tensor_reduce(out=vsum[:], in_=vsums[:], axis=AX.X, op=ALU.add)
         sums(NCH - 1)
-        nc.vector.tensor_copy(out=tsum[:], in_=banks[7][:, 0:1])
+        nc.vector.tensor_scalar(out=tsum[:], in0=banks[7][:, 0:1], scalar1=vsum[:], scalar2=None, op0=ALU.add)
         nc.tensor.matmul(out=banks[6][:, 0:1], lhsT=ones_f[:], rhs=tsum[:], start=True, stop=True)
         nc.vector.tensor_scalar(out=thr[:], in0=banks[6][:, 0:1], scalar1=2.0**-100, scalar2=None, op0=ALU.max)
         nc.vector.tensor_scalar(

@@ -21,9 +21,7 @@ NI = TOKENS // P
 NCH = OUTF // P
 MAG_BITS = 0x7FFF7FFF
 TOP_BITS = -1073692672
-UPPER_HALF = -65536
-HALF_STEP = 32768
-JUST_UNDER_TWO = 2.0 - 2.0**-8
+SCALE = (2.0 - 2.0**-8) * OUTF * K - 4.0
 NAT_BUFS = 12
 FIRST_PIECES = 4
 NCOL = 56
@@ -31,8 +29,8 @@ BLOCK_CHUNKS = (1, 1, 2, 2, 2, 2, 2, 2, 2)
 V_SLICE = 512
 HEAD_WARM = 2
 PAIRS = ((0, 1), (2, 3), (4, 5))
-LATE_PAIRS = ((2, 3), (6, 7), (4, 5))
-X_GROUPS = 10
+X_PAIRS = ((2, 3), (4, 5), (6, 7), (4, 5), (6, 7), (4, 5), (6, 7), (4, 5))
+MX_BANKS = 4
 
 
 def tile_ternarylinear_kernel(tc, x, weight, out):
@@ -61,7 +59,6 @@ def tile_ternarylinear_kernel(tc, x, weight, out):
         tsum = const.tile([P, 1], F32, name="tsum")
         vsums = const.tile([P, NCH], F32, name="vsums")
         vsum = const.tile([P, 1], F32, name="vsum")
-        thr = const.tile([P, 1], F32, name="thr")
         inv = const.tile([P, 1], F32, name="inv")
 
         raw = [keep.tile([P, 8 * width[b]], F32, name="raw%d" % b, align_bytes=64) for b in range(nb)]
@@ -169,63 +166,59 @@ def tile_ternarylinear_kernel(tc, x, weight, out):
         vector_sum(NCH - 1)
         nc.vector.tensor_reduce(out=vsum[:], in_=vsums[:], axis=AX.X, op=ALU.add)
         sums(NCH - 1)
-        nc.vector.tensor_scalar(out=tsum[:], in0=banks[7][:, 0:1], scalar1=vsum[:], scalar2=None, op0=ALU.add)
-        nc.tensor.matmul(out=banks[6][:, 0:1], lhsT=ones_f[:], rhs=tsum[:], start=True, stop=True)
-        nc.vector.tensor_scalar(out=thr[:], in0=banks[6][:, 0:1], scalar1=2.0**-100, scalar2=None, op0=ALU.max)
+        w_turn(NCH - 1, PAIRS[(NCH - 1) % 3])
         nc.vector.tensor_scalar(
-            out=thr[:].bitcast(I32),
-            in0=thr[:].bitcast(I32),
-            scalar1=UPPER_HALF,
-            scalar2=HALF_STEP,
-            op0=ALU.bitwise_and,
-            op1=ALU.bitwise_or,
+            out=tsum[:], in0=banks[7][:, 0:1], scalar1=vsum[:], scalar2=2.0**-100, op0=ALU.add, op1=ALU.max
         )
-        nc.vector.reciprocal(out=inv[:], in_=thr[:])
+        nc.tensor.matmul(out=banks[6][:, 0:1], lhsT=ones_f[:], rhs=tsum[:], start=True, stop=True)
+        nc.vector.reciprocal(out=inv[:], in_=banks[6][:, 0:1])
 
         xg = {}
-        n_turn = [0]
         x_ready = []
         b_ready = []
         n_group = [0]
 
         def x_turn(i):
-            pair = LATE_PAIRS[n_turn[0] % 3]
-            n_turn[0] += 1
+            pair = X_PAIRS[i]
             transposes(tiles[NCH + i], pair)
             xg[i] = xgs.tile([P, 1024], F32, name="xgt", tag="xg", align_bytes=64)
             exits(xg[i][:].rearrange("p (g o u) -> p g o u", g=NG, u=2), pair, nc.scalar.copy)
 
-        def group(b, i):
-            w = width[b]
-            bank = banks[n_group[0] % (2 if n_group[0] < X_GROUPS else 4)]
+        def group(b, i, c0, w):
+            bank = banks[n_group[0] % MX_BANKS]
             for g in range(NG):
                 nc.tensor.matmul_mx(
                     out=bank[:, 0:w],
                     lhsT=xcod[i][:, g * P : (g + 1) * P].bitcast(FP8X4),
                     lhsT_scale=xpl[i][:, g * P : (g + 1) * P],
-                    rhs=wcod[b][:, g * w : (g + 1) * w].bitcast(FP8X4),
-                    rhs_scale=wpl[b][:, g * w : (g + 1) * w],
+                    rhs=wcod[b][:, g * width[b] + c0 : g * width[b] + c0 + w].bitcast(FP8X4),
+                    rhs_scale=wpl[b][:, g * width[b] + c0 : g * width[b] + c0 + w],
                     start=(g == 0),
                     stop=(g == NG - 1),
                 )
             st = stg.tile([P, 256], F32, name="stage")
-            if b == nb - 1 and i % 2 == 1:
+            if b == nb - 1 and n_group[0] % 2 == 1:
                 nc.vector.tensor_scalar(out=st[:, 0:w], in0=bank[:, 0:w], scalar1=0.5, scalar2=None, op0=ALU.mult)
             else:
                 nc.scalar.activation(out=st[:, 0:w], in_=bank[:, 0:w], func=ACT.Copy, scale=0.5)
-            nc.sync.dma_start(out=out[i * P : (i + 1) * P, first[b] * P : first[b] * P + w], in_=st[:, 0:w])
+            nc.sync.dma_start(out=out[i * P : (i + 1) * P, first[b] * P + c0 : first[b] * P + c0 + w], in_=st[:, 0:w])
             n_group[0] += 1
+
+        def groups(b, i):
+            n = 2 if (b, i) == (nb - 1, NI - 1) else 1
+            for q in range(n):
+                group(b, i, q * width[b] // n, width[b] // n)
 
         def x_quant(i):
             nc.vector.quantize_mx(out=xcod[i][:].bitcast(FP8X4), scales=xpl[i][:], in_=xg[i][:].bitcast(BF16))
             x_ready.append(i)
             for b in b_ready:
-                group(b, i)
+                groups(b, i)
 
         def scale(b):
             v = raw[b][:].bitcast(BF16)
             nc.vector.tensor_scalar(
-                out=v, in0=v, scalar1=inv[:], scalar2=JUST_UNDER_TWO * (OUTF * K), op0=ALU.mult, op1=ALU.mult
+                out=v, in0=v, scalar1=inv[:], scalar2=SCALE, op0=ALU.mult, op1=ALU.mult
             )
 
         def cut(b):
@@ -236,30 +229,23 @@ def tile_ternarylinear_kernel(tc, x, weight, out):
             nc.vector.quantize_mx(out=wcod[b][:].bitcast(FP8X4), scales=wpl[b][:], in_=raw[b][:].bitcast(BF16))
             b_ready.append(b)
             for i in x_ready:
-                group(b, i)
+                groups(b, i)
 
-        warm(1)
         x_turn(0)
-        warm(1)
         x_turn(1)
-        warm(1)
-        w_turn(NCH - 1, LATE_PAIRS[2])
-        n_turn[0] += 1
-        warm(1)
         scale(0)
         cut(0)
         x_turn(2)
-        warm(1)
+        scale(1)
+        x_turn(3)
         x_quant(0)
         t_quant(0)
-        x_turn(3)
-        scale(1)
+        cut(1)
         x_quant(1)
         x_turn(4)
-        cut(1)
+        t_quant(1)
         x_quant(2)
         x_turn(5)
-        t_quant(1)
         scale(2)
         x_quant(3)
         x_turn(6)

from contextlib import ExitStack

import concourse.mybir as mybir
from concourse.masks import make_identity

F32 = mybir.dt.float32
BF16 = mybir.dt.bfloat16
I32 = mybir.dt.int32
U32 = mybir.dt.uint32
U8 = mybir.dt.uint8
FP8X4 = mybir.dt.float8_e4m3fn_x4
ALU = mybir.AluOpType
AX = mybir.AxisListType
ACT = mybir.ActivationFunctionType

P = 128
TOKENS, K, OUTF = 1024, 2048, 2048
FLOPS = 2 * TOKENS * K * OUTF
NG = K // 512
NI = TOKENS // P
NCH = OUTF // P
MAG_BITS = 0x7FFF7FFF
TOP_BITS = -1073692672
SCALE = (2.0 - 2.0**-8) * OUTF * K - 4.0
NAT_BUFS = 12
FIRST_PIECES = 4
NCOL = 56
BLOCK_CHUNKS = (1, 1, 2, 2, 2, 2, 2, 2, 2)
V_SLICE = 512
HEAD_WARM = 2
PAIRS = ((0, 1), (2, 3), (4, 5))
X_PAIRS = ((2, 3), (4, 5), (6, 7), (4, 5), (6, 7), (4, 5), (6, 7), (4, 5))
MX_BANKS = 4


def tile_ternarylinear_kernel(tc, x, weight, out):
    nc = tc.nc
    nb = len(BLOCK_CHUNKS)
    first = [sum(BLOCK_CHUNKS[:b]) for b in range(nb)]
    width = [P * n for n in BLOCK_CHUNKS]
    with ExitStack() as ctx:
        ctx.enter_context(tc.manual_schedule())
        const = ctx.enter_context(tc.tile_pool(name="const", bufs=1))
        keep = ctx.enter_context(tc.tile_pool(name="keep", bufs=1))
        nat = ctx.enter_context(tc.tile_pool(name="nat", bufs=NAT_BUFS))
        mags = ctx.enter_context(tc.tile_pool(name="mags", bufs=3))
        xgs = ctx.enter_context(tc.tile_pool(name="xgs", bufs=3))
        stg = ctx.enter_context(tc.tile_pool(name="stg", bufs=8))
        psum = ctx.enter_context(tc.psum_pool(name="psum", bufs=1))

        ident = const.tile([P, P], F32, name="ident")
        make_identity(nc, ident[:])
        ones_bf = const.tile([P, 512], BF16, name="ones_bf", align_bytes=64)
        nc.vector.memset(ones_bf[:], 1.0)
        ones_f = const.tile([P, P], F32, name="ones_f")
        nc.vector.memset(ones_f[:], 1.0)
        junk = const.tile([P, 1], F32, name="junk")
        nc.scalar.activation(out=junk[:], in_=ones_f[:, 0:1], func=ACT.Copy)
        tsum = const.tile([P, 1], F32, name="tsum")
        vsums = const.tile([P, NCH], F32, name="vsums")
        vsum = const.tile([P, 1], F32, name="vsum")
        inv = const.tile([P, 1], F32, name="inv")

        raw = [keep.tile([P, 8 * width[b]], F32, name="raw%d" % b, align_bytes=64) for b in range(nb)]
        wcod = [keep.tile([P, NG * width[b]], U32, name="wcod%d" % b, align_bytes=64) for b in range(nb)]
        wpl = [keep.tile([P, NG * width[b]], U8, name="wpl%d" % b, align_bytes=64) for b in range(nb)]
        xcod = [keep.tile([P, 512], U32, name="xcod%d" % i, align_bytes=64) for i in range(NI)]
        xpl = [keep.tile([P, 512], U8, name="xpl%d" % i, align_bytes=64) for i in range(NI)]
        banks = [psum.tile([P, 512], F32, name="bank%d" % b) for b in range(8)]

        steps = []
        b = 0
        while b < nb:
            if BLOCK_CHUNKS[b] == 1:
                steps.append((b, 0))
                b += 1
            elif b + 1 < nb:
                steps.extend([(b, 0), (b + 1, 0), (b, 1), (b + 1, 1)])
                b += 2
            else:
                steps.extend([(b, 0), (b, 1)])
                b += 1

        def rows_of(s):
            if s < NCH:
                c = first[steps[s][0]] + steps[s][1]
                return weight[c * P : (c + 1) * P, :]
            return x[(s - NCH) * P : (s - NCH + 1) * P, :]

        tiles = {}

        def load(s):
            tiles[s] = nat.tile([P, K], BF16, name="natt", tag="nat", align_bytes=64)
            pieces = FIRST_PIECES if s == 0 else 1
            for j in range(pieces):
                cols = slice(j * K // pieces, (j + 1) * K // pieces)
                nc.sync.dma_start(out=tiles[s][:, cols], in_=rows_of(s)[:, cols])

        def transposes(src, pair):
            words = src[:].bitcast(F32)
            for j in range(8):
                nc.tensor.transpose(
                    banks[pair[j // 4]][:, (j % 4) * P : (j % 4 + 1) * P], words[:, j * P : (j + 1) * P], ident[:]
                )

        def exits(dst, pair, copy):
            for h in range(2):
                copy(
                    out=dst[:, 2 * h : 2 * h + 2, :, :],
                    in_=banks[pair[h]][:].rearrange("p (g u o) -> p g o u", g=2, u=2),
                )

        magn = {}

        def magnitude(s):
            magn[s] = mags.tile([P, K], BF16, name="magt", tag="mag", align_bytes=64)
            nc.vector.tensor_scalar(
                out=magn[s][:].bitcast(I32),
                in0=tiles[s][:].bitcast(I32),
                scalar1=MAG_BITS,
                scalar2=None,
                op0=ALU.bitwise_and,
            )

        def vector_sum(s):
            part = magn[s][:, K - V_SLICE : K]
            nc.vector.tensor_scalar(
                out=part, in0=part, scalar1=1.0, scalar2=None, op0=ALU.mult, op1=ALU.add, accum_out=vsums[:, s : s + 1]
            )

        def sums(s):
            for j in range((K - V_SLICE) // P):
                nc.tensor.matmul(
                    out=banks[7][:, 0:NCOL],
                    lhsT=magn[s][:, j * P : (j + 1) * P],
                    rhs=ones_bf[:, 0:NCOL],
                    start=(s == 0 and j == 0),
                    stop=(s == NCH - 1 and j == (K - V_SLICE) // P - 1),
                )

        def warm(n):
            for j in range(n):
                nc.tensor.matmul(out=banks[1][:], lhsT=ones_bf[:, 0:P], rhs=ones_bf[:], start=True, stop=True)

        warm(HEAD_WARM)
        for s in range(NAT_BUFS):
            load(s)
        def w_turn(s, pair):
            b, cc = steps[s]
            transposes(tiles[s], pair)
            exits(
                raw[b][:].rearrange("p (g o u) -> p g o u", g=NG, u=2)[:, :, cc * P : (cc + 1) * P, :],
                pair,
                nc.scalar.copy,
            )

        for s in range(NCH):
            if s < NCH - 1:
                w_turn(s, PAIRS[s % 3])
            magnitude(s)
            if s >= 1:
                vector_sum(s - 1)
                sums(s - 1)
            if s + NAT_BUFS < NCH + NI:
                load(s + NAT_BUFS)
        vector_sum(NCH - 1)
        nc.vector.tensor_reduce(out=vsum[:], in_=vsums[:], axis=AX.X, op=ALU.add)
        sums(NCH - 1)
        w_turn(NCH - 1, PAIRS[(NCH - 1) % 3])
        nc.vector.tensor_scalar(
            out=tsum[:], in0=banks[7][:, 0:1], scalar1=vsum[:], scalar2=2.0**-100, op0=ALU.add, op1=ALU.max
        )
        nc.tensor.matmul(out=banks[6][:, 0:1], lhsT=ones_f[:], rhs=tsum[:], start=True, stop=True)
        nc.vector.reciprocal(out=inv[:], in_=banks[6][:, 0:1])

        xg = {}
        x_ready = []
        b_ready = []
        n_group = [0]

        def x_turn(i):
            pair = X_PAIRS[i]
            transposes(tiles[NCH + i], pair)
            xg[i] = xgs.tile([P, 1024], F32, name="xgt", tag="xg", align_bytes=64)
            exits(xg[i][:].rearrange("p (g o u) -> p g o u", g=NG, u=2), pair, nc.scalar.copy)

        def group(b, i, c0, w):
            bank = banks[n_group[0] % MX_BANKS]
            for g in range(NG):
                nc.tensor.matmul_mx(
                    out=bank[:, 0:w],
                    lhsT=xcod[i][:, g * P : (g + 1) * P].bitcast(FP8X4),
                    lhsT_scale=xpl[i][:, g * P : (g + 1) * P],
                    rhs=wcod[b][:, g * width[b] + c0 : g * width[b] + c0 + w].bitcast(FP8X4),
                    rhs_scale=wpl[b][:, g * width[b] + c0 : g * width[b] + c0 + w],
                    start=(g == 0),
                    stop=(g == NG - 1),
                )
            st = stg.tile([P, 256], F32, name="stage")
            if b == nb - 1 and n_group[0] % 2 == 1:
                nc.vector.tensor_scalar(out=st[:, 0:w], in0=bank[:, 0:w], scalar1=0.5, scalar2=None, op0=ALU.mult)
            else:
                nc.scalar.activation(out=st[:, 0:w], in_=bank[:, 0:w], func=ACT.Copy, scale=0.5)
            nc.sync.dma_start(out=out[i * P : (i + 1) * P, first[b] * P + c0 : first[b] * P + c0 + w], in_=st[:, 0:w])
            n_group[0] += 1

        def groups(b, i):
            n = 2 if (b, i) == (nb - 1, NI - 1) else 1
            for q in range(n):
                group(b, i, q * width[b] // n, width[b] // n)

        def x_quant(i):
            nc.vector.quantize_mx(out=xcod[i][:].bitcast(FP8X4), scales=xpl[i][:], in_=xg[i][:].bitcast(BF16))
            x_ready.append(i)
            for b in b_ready:
                groups(b, i)

        def scale(b):
            v = raw[b][:].bitcast(BF16)
            nc.vector.tensor_scalar(
                out=v, in0=v, scalar1=inv[:], scalar2=SCALE, op0=ALU.mult, op1=ALU.mult
            )

        def cut(b):
            r = raw[b][:].bitcast(I32)
            nc.vector.tensor_scalar(out=r, in0=r, scalar1=TOP_BITS, scalar2=None, op0=ALU.bitwise_and)

        def t_quant(b):
            nc.vector.quantize_mx(out=wcod[b][:].bitcast(FP8X4), scales=wpl[b][:], in_=raw[b][:].bitcast(BF16))
            b_ready.append(b)
            for i in x_ready:
                groups(b, i)

        x_turn(0)
        x_turn(1)
        scale(0)
        cut(0)
        x_turn(2)
        scale(1)
        x_turn(3)
        x_quant(0)
        t_quant(0)
        cut(1)
        x_quant(1)
        x_turn(4)
        t_quant(1)
        x_quant(2)
        x_turn(5)
        scale(2)
        x_quant(3)
        x_turn(6)
        cut(2)
        x_quant(4)
        x_turn(7)
        t_quant(2)
        scale(3)
        x_quant(5)
        cut(3)
        x_quant(6)
        t_quant(3)
        scale(4)
        x_quant(7)
        for b in range(4, nb):
            cut(b)
            if b + 1 < nb:
                scale(b + 1)
            t_quant(b)
